import numpy as np
import ml_dtypes

BF16 = ml_dtypes.bfloat16


def bf(x):
    return np.asarray(x, np.float32).astype(BF16)


def f32(x):
    return np.asarray(x, np.float32)


def f64(x):
    return np.asarray(x).astype(np.float64)


def striped(idx):
    return np.tile(idx.reshape(-1, 16).T, (8, 1))


C, S, N = 512, 2048, 256


def sigmoid(v):
    return 1.0 / (1.0 + np.exp(-v))


def setup_inputs():
    return {
        "emb": f32(np.random.standard_normal((C, S))),
        "h": bf(np.random.standard_normal((C, N))),
        "w0": bf(np.random.standard_normal((C, C)) / np.sqrt(C)),
        "b0": f32(0.1 * np.random.standard_normal((C, 1))),
        "w1": bf(np.random.standard_normal((C, C)) / np.sqrt(C)),
        "b1": f32(0.1 * np.random.standard_normal((C, 1))),
        "offs": striped(np.random.permutation(np.tile(np.arange(S), 2))[:N]),
    }


def reference(emb, h, w0, b0, w1, b1, offs):
    idx = offs[:16].T.reshape(-1)
    q0 = 2.0 * sigmoid(f64(w0).T @ f64(h) + f64(b0))
    x1 = f64(emb)[:, idx] * q0
    q1 = 2.0 * sigmoid(f64(w1).T @ x1 + f64(b1))
    h1 = q1 * f64(h)
    return np.concatenate([x1, h1], axis=0)

@@ -1,0 +1,83 @@
+import concourse.mybir as mybir
+
+F32, BF16, U16 = mybir.dt.float32, mybir.dt.bfloat16, mybir.dt.uint16
+MULT = mybir.AluOpType.mult
+SIGMOID = mybir.ActivationFunctionType.Sigmoid
+
+P = 128
+C = 512
+S = 2048
+N = 256
+BLOCKS = C // P
+
+FLOPS = 2 * (2 * C * C * N)
+
+
+def tile_luongattndecodermoglstm_kernel(tc, emb, h, w0, b0, w1, b1, offs, out):
+    nc = tc.nc
+    with (
+        tc.tile_pool(name="held", bufs=1) as held,
+        tc.tile_pool(name="per_block", bufs=BLOCKS) as per_block,
+        tc.psum_pool(name="sums0", bufs=2) as sums0,
+        tc.psum_pool(name="sums1", bufs=1) as sums1,
+    ):
+        offsets = held.tile([P, N // 16], U16, name="offsets")
+        nc.sync.dma_start(offsets[:], offs)
+
+        h_sb = held.tile([P, BLOCKS, N], BF16, name="h_sb")
+        nc.sync.dma_start(h_sb[:], h.rearrange("(b p) j -> p b j", p=P))
+        w0_sb = held.tile([P, BLOCKS, C], BF16, name="w0_sb")
+        nc.sync.dma_start(w0_sb[:], w0.rearrange("(b p) c -> p b c", p=P))
+
+        b0_sb = held.tile([P, BLOCKS], F32, name="b0_sb")
+        b1_sb = held.tile([P, BLOCKS], F32, name="b1_sb")
+        with nc.allow_non_contiguous_dma(reason="512 bias values, one to a partition"):
+            nc.scalar.dma_start(b0_sb[:], b0.rearrange("(b p) o -> p (b o)", p=P))
+            nc.scalar.dma_start(b1_sb[:], b1.rearrange("(b p) o -> p (b o)", p=P))
+
+        emb_sb = [held.tile([P, S], F32, name=f"emb{b}") for b in range(BLOCKS)]
+        w1_sb = held.tile([P, BLOCKS, C], BF16, name="w1_sb")
+        nc.sync.dma_start(emb_sb[0][:], emb[0:P, :])
+        nc.sync.dma_start(w1_sb[:], w1.rearrange("(b p) c -> p b c", p=P))
+        for b in range(1, BLOCKS):
+            nc.sync.dma_start(emb_sb[b][:], emb[b * P : (b + 1) * P, :])
+
+        q0 = []
+        for c in range(BLOCKS):
+            sum0 = sums0.tile([P, N], F32, name="sum0")
+            for k in range(BLOCKS):
+                nc.tensor.matmul(
+                    sum0[:],
+                    w0_sb[:, k, c * P : (c + 1) * P],
+                    h_sb[:, k, :],
+                    start=(k == 0),
+                    stop=(k == BLOCKS - 1),
+                )
+            sig0 = per_block.tile([P, N], F32, name="sig0")
+            nc.scalar.activation(sig0[:], sum0[:], SIGMOID, bias=b0_sb[:, c : c + 1])
+            q0_c = per_block.tile([P, N], F32, name="q0_c")
+            nc.vector.tensor_scalar_mul(q0_c[:], sig0[:], 2.0)
+            q0.append(q0_c)
+
+        sum1 = [sums1.tile([P, N], F32, name=f"sum1_{c}") for c in range(BLOCKS)]
+        for k in range(BLOCKS):
+            x1 = per_block.tile([P, N], F32, name="x1")
+            nc.vector.tensor_tensor(x1[:], emb_sb[k][:].indirect(offsets[:]), q0[k][:], MULT)
+            nc.sync.dma_start(out[k * P : (k + 1) * P, :], x1[:])
+            x1_bf = per_block.tile([P, N], BF16, name="x1_bf")
+            nc.vector.tensor_copy(x1_bf[:], x1[:])
+            for c in range(BLOCKS):
+                nc.tensor.matmul(
+                    sum1[c][:],
+                    w1_sb[:, k, c * P : (c + 1) * P],
+                    x1_bf[:],
+                    start=(k == 0),
+                    stop=(k == BLOCKS - 1),
+                )
+
+        for c in range(BLOCKS):
+            sig1 = per_block.tile([P, N], F32, name="sig1")
+            nc.scalar.activation(sig1[:], sum1[c][:], SIGMOID, bias=b1_sb[:, c : c + 1])
+            h1 = per_block.tile([P, N], F32, name="h1")
+            nc.vector.scalar_tensor_tensor(h1[:], sig1[:], 2.0, h_sb[:, c, :], MULT, MULT)
+            nc.sync.dma_start(out[C + c * P : C + (c + 1) * P, :], h1[:])

@@ -25,22 +25,24 @@ def tile_luongattndecodermoglstm_kernel(tc, emb, h, w0, b0, w1, b1, offs, out):
         nc.sync.dma_start(offsets[:], offs)
 
         h_sb = held.tile([P, BLOCKS, N], BF16, name="h_sb")
-        nc.sync.dma_start(h_sb[:], h.rearrange("(b p) j -> p b j", p=P))
-        w0_sb = held.tile([P, BLOCKS, C], BF16, name="w0_sb")
-        nc.sync.dma_start(w0_sb[:], w0.rearrange("(b p) c -> p b c", p=P))
+        nc.sync.dma_start(h_sb[:], h.rearrange("(p b) j -> p b j", b=BLOCKS))
+        w0_sb = held.tile([P, BLOCKS, P, BLOCKS], BF16, name="w0_sb")
+        nc.sync.dma_start(w0_sb[:], w0.rearrange("(p k) (m c) -> p k m c", k=BLOCKS, c=BLOCKS))
 
         b0_sb = held.tile([P, BLOCKS], F32, name="b0_sb")
         b1_sb = held.tile([P, BLOCKS], F32, name="b1_sb")
-        with nc.allow_non_contiguous_dma(reason="512 bias values, one to a partition"):
-            nc.scalar.dma_start(b0_sb[:], b0.rearrange("(b p) o -> p (b o)", p=P))
-            nc.scalar.dma_start(b1_sb[:], b1.rearrange("(b p) o -> p (b o)", p=P))
+        nc.scalar.dma_start(b0_sb[:], b0.rearrange("(p b) o -> p (b o)", b=BLOCKS))
+        nc.scalar.dma_start(b1_sb[:], b1.rearrange("(p b) o -> p (b o)", b=BLOCKS))
 
+        emb_blocks = emb.rearrange("(p b) s -> p b s", b=BLOCKS)
         emb_sb = [held.tile([P, S], F32, name=f"emb{b}") for b in range(BLOCKS)]
-        w1_sb = held.tile([P, BLOCKS, C], BF16, name="w1_sb")
-        nc.sync.dma_start(emb_sb[0][:], emb[0:P, :])
-        nc.sync.dma_start(w1_sb[:], w1.rearrange("(b p) c -> p b c", p=P))
+        w1_sb = held.tile([P, BLOCKS, P, BLOCKS], BF16, name="w1_sb")
+        nc.sync.dma_start(emb_sb[0][:], emb_blocks[:, 0, :])
+        nc.sync.dma_start(w1_sb[:], w1.rearrange("(p k) (m c) -> p k m c", k=BLOCKS, c=BLOCKS))
         for b in range(1, BLOCKS):
-            nc.sync.dma_start(emb_sb[b][:], emb[b * P : (b + 1) * P, :])
+            nc.sync.dma_start(emb_sb[b][:], emb_blocks[:, b, :])
+
+        out_blocks = out.rearrange("(r p b) j -> r p b j", r=2, b=BLOCKS)
 
         q0 = []
         for c in range(BLOCKS):
@@ -48,7 +50,7 @@ def tile_luongattndecodermoglstm_kernel(tc, emb, h, w0, b0, w1, b1, offs, out):
             for k in range(BLOCKS):
                 nc.tensor.matmul(
                     sum0[:],
-                    w0_sb[:, k, c * P : (c + 1) * P],
+                    w0_sb[:, k, :, c],
                     h_sb[:, k, :],
                     start=(k == 0),
                     stop=(k == BLOCKS - 1),
@@ -63,13 +65,13 @@ def tile_luongattndecodermoglstm_kernel(tc, emb, h, w0, b0, w1, b1, offs, out):
         for k in range(BLOCKS):
             x1 = per_block.tile([P, N], F32, name="x1")
             nc.vector.tensor_tensor(x1[:], emb_sb[k][:].indirect(offsets[:]), q0[k][:], MULT)
-            nc.sync.dma_start(out[k * P : (k + 1) * P, :], x1[:])
+            nc.sync.dma_start(out_blocks[0, :, k, :], x1[:])
             x1_bf = per_block.tile([P, N], BF16, name="x1_bf")
             nc.vector.tensor_copy(x1_bf[:], x1[:])
             for c in range(BLOCKS):
                 nc.tensor.matmul(
                     sum1[c][:],
-                    w1_sb[:, k, c * P : (c + 1) * P],
+                    w1_sb[:, k, :, c],
                     x1_bf[:],
                     start=(k == 0),
                     stop=(k == BLOCKS - 1),
@@ -80,4 +82,4 @@ def tile_luongattndecodermoglstm_kernel(tc, emb, h, w0, b0, w1, b1, offs, out):
             nc.scalar.activation(sig1[:], sum1[c][:], SIGMOID, bias=b1_sb[:, c : c + 1])
             h1 = per_block.tile([P, N], F32, name="h1")
             nc.vector.scalar_tensor_tensor(h1[:], sig1[:], 2.0, h_sb[:, c, :], MULT, MULT)
-            nc.sync.dma_start(out[C + c * P : C + (c + 1) * P, :], h1[:])
+            nc.sync.dma_start(out_blocks[1, :, c, :], h1[:])

@@ -37,10 +37,13 @@ def tile_luongattndecodermoglstm_kernel(tc, emb, h, w0, b0, w1, b1, offs, out):
         emb_blocks = emb.rearrange("(p b) s -> p b s", b=BLOCKS)
         emb_sb = [held.tile([P, S], F32, name=f"emb{b}") for b in range(BLOCKS)]
         w1_sb = held.tile([P, BLOCKS, P, BLOCKS], BF16, name="w1_sb")
+        w1_blocks = w1.rearrange("(p k) (m c) -> p k m c", k=BLOCKS, c=BLOCKS)
+        LAST = BLOCKS - 1
         nc.sync.dma_start(emb_sb[0][:], emb_blocks[:, 0, :])
-        nc.sync.dma_start(w1_sb[:], w1.rearrange("(p k) (m c) -> p k m c", k=BLOCKS, c=BLOCKS))
+        nc.sync.dma_start(w1_sb[:, 0:LAST], w1_blocks[:, 0:LAST])
         for b in range(1, BLOCKS):
             nc.sync.dma_start(emb_sb[b][:], emb_blocks[:, b, :])
+        nc.sync.dma_start(w1_sb[:, LAST], w1_blocks[:, LAST])
 
         out_blocks = out.rearrange("(r p b) j -> r p b j", r=2, b=BLOCKS)
 

@@ -9,6 +9,8 @@ C = 512
 S = 2048
 N = 256
 BLOCKS = C // P
+PIECES = 2
+W = N // PIECES
 
 FLOPS = 2 * (2 * C * C * N)
 
@@ -18,8 +20,7 @@ def tile_luongattndecodermoglstm_kernel(tc, emb, h, w0, b0, w1, b1, offs, out):
     with (
         tc.tile_pool(name="held", bufs=1) as held,
         tc.tile_pool(name="per_block", bufs=BLOCKS) as per_block,
-        tc.psum_pool(name="sums0", bufs=2) as sums0,
-        tc.psum_pool(name="sums1", bufs=1) as sums1,
+        tc.tile_pool(name="per_piece", bufs=BLOCKS * PIECES) as per_piece,
     ):
         offsets = held.tile([P, N // 16], U16, name="offsets")
         nc.sync.dma_start(offsets[:], offs)
@@ -48,41 +49,51 @@ def tile_luongattndecodermoglstm_kernel(tc, emb, h, w0, b0, w1, b1, offs, out):
         out_blocks = out.rearrange("(r p b) j -> r p b j", r=2, b=BLOCKS)
 
         q0 = []
-        for c in range(BLOCKS):
-            sum0 = sums0.tile([P, N], F32, name="sum0")
-            for k in range(BLOCKS):
-                nc.tensor.matmul(
-                    sum0[:],
-                    w0_sb[:, k, :, c],
-                    h_sb[:, k, :],
-                    start=(k == 0),
-                    stop=(k == BLOCKS - 1),
-                )
-            sig0 = per_block.tile([P, N], F32, name="sig0")
-            nc.scalar.activation(sig0[:], sum0[:], SIGMOID, bias=b0_sb[:, c : c + 1])
-            q0_c = per_block.tile([P, N], F32, name="q0_c")
-            nc.vector.tensor_scalar_mul(q0_c[:], sig0[:], 2.0)
-            q0.append(q0_c)
-
-        sum1 = [sums1.tile([P, N], F32, name=f"sum1_{c}") for c in range(BLOCKS)]
-        for k in range(BLOCKS):
-            x1 = per_block.tile([P, N], F32, name="x1")
-            nc.vector.tensor_tensor(x1[:], emb_sb[k][:].indirect(offsets[:]), q0[k][:], MULT)
-            nc.sync.dma_start(out_blocks[0, :, k, :], x1[:])
-            x1_bf = per_block.tile([P, N], BF16, name="x1_bf")
-            nc.vector.tensor_copy(x1_bf[:], x1[:])
+        with tc.psum_pool(name="sums0", bufs=2) as sums0:
             for c in range(BLOCKS):
-                nc.tensor.matmul(
-                    sum1[c][:],
-                    w1_sb[:, k, :, c],
-                    x1_bf[:],
-                    start=(k == 0),
-                    stop=(k == BLOCKS - 1),
-                )
+                sum0 = sums0.tile([P, N], F32, name="sum0")
+                for k in range(BLOCKS):
+                    nc.tensor.matmul(
+                        sum0[:],
+                        w0_sb[:, k, :, c],
+                        h_sb[:, k, :],
+                        start=(k == 0),
+                        stop=(k == BLOCKS - 1),
+                    )
+                sig0 = per_block.tile([P, N], F32, name="sig0")
+                nc.scalar.activation(sig0[:], sum0[:], SIGMOID, bias=b0_sb[:, c : c + 1])
+                q0_c = per_block.tile([P, N], F32, name="q0_c")
+                nc.vector.tensor_scalar_mul(q0_c[:], sig0[:], 2.0)
+                q0.append(q0_c)
 
-        for c in range(BLOCKS):
-            sig1 = per_block.tile([P, N], F32, name="sig1")
-            nc.scalar.activation(sig1[:], sum1[c][:], SIGMOID, bias=b1_sb[:, c : c + 1])
-            h1 = per_block.tile([P, N], F32, name="h1")
-            nc.vector.scalar_tensor_tensor(h1[:], sig1[:], 2.0, h_sb[:, c, :], MULT, MULT)
-            nc.sync.dma_start(out_blocks[1, :, c, :], h1[:])
+        with tc.psum_pool(name="sums1", bufs=1) as sums1:
+            sum1 = [
+                [sums1.tile([P, W], F32, name=f"sum1_{c}_{i}") for i in range(PIECES)]
+                for c in range(BLOCKS)
+            ]
+            for k in range(BLOCKS):
+                x1 = per_block.tile([P, N], F32, name="x1")
+                x1_bf = per_block.tile([P, N], BF16, name="x1_bf")
+                for i in range(PIECES):
+                    piece = slice(i * W, (i + 1) * W)
+                    looked_up = emb_sb[k][:].indirect(offsets[:, i * W // 16 : (i + 1) * W // 16])
+                    nc.vector.tensor_tensor(x1[:, piece], looked_up, q0[k][:, piece], MULT)
+                    nc.vector.tensor_copy(x1_bf[:, piece], x1[:, piece])
+                    for c in range(BLOCKS):
+                        nc.tensor.matmul(
+                            sum1[c][i][:],
+                            w1_sb[:, k, :, c],
+                            x1_bf[:, piece],
+                            start=(k == 0),
+                            stop=(k == BLOCKS - 1),
+                        )
+                nc.sync.dma_start(out_blocks[0, :, k, :], x1[:])
+
+            for i in range(PIECES):
+                piece = slice(i * W, (i + 1) * W)
+                for c in range(BLOCKS):
+                    sig1 = per_piece.tile([P, W], F32, name="sig1")
+                    nc.scalar.activation(sig1[:], sum1[c][i][:], SIGMOID, bias=b1_sb[:, c : c + 1])
+                    h1 = per_piece.tile([P, W], F32, name="h1")
+                    nc.vector.scalar_tensor_tensor(h1[:], sig1[:], 2.0, h_sb[:, c, piece], MULT, MULT)
+                    nc.sync.dma_start(out_blocks[1, :, c, piece], h1[:])

@@ -10,7 +10,7 @@ S = 2048
 N = 256
 BLOCKS = C // P
 PIECES = 2
-W = N // PIECES
+CUTS = [0, N // 4, N]
 
 FLOPS = 2 * (2 * C * C * N)
 
@@ -68,15 +68,15 @@ def tile_luongattndecodermoglstm_kernel(tc, emb, h, w0, b0, w1, b1, offs, out):
 
         with tc.psum_pool(name="sums1", bufs=1) as sums1:
             sum1 = [
-                [sums1.tile([P, W], F32, name=f"sum1_{c}_{i}") for i in range(PIECES)]
+                [sums1.tile([P, CUTS[i + 1] - CUTS[i]], F32, name=f"sum1_{c}_{i}") for i in range(PIECES)]
                 for c in range(BLOCKS)
             ]
             for k in range(BLOCKS):
                 x1 = per_block.tile([P, N], F32, name="x1")
                 x1_bf = per_block.tile([P, N], BF16, name="x1_bf")
                 for i in range(PIECES):
-                    piece = slice(i * W, (i + 1) * W)
-                    looked_up = emb_sb[k][:].indirect(offsets[:, i * W // 16 : (i + 1) * W // 16])
+                    piece = slice(CUTS[i], CUTS[i + 1])
+                    looked_up = emb_sb[k][:].indirect(offsets[:, CUTS[i] // 16 : CUTS[i + 1] // 16])
                     nc.vector.tensor_tensor(x1[:, piece], looked_up, q0[k][:, piece], MULT)
                     nc.vector.tensor_copy(x1_bf[:, piece], x1[:, piece])
                     for c in range(BLOCKS):
@@ -90,10 +90,10 @@ def tile_luongattndecodermoglstm_kernel(tc, emb, h, w0, b0, w1, b1, offs, out):
                 nc.sync.dma_start(out_blocks[0, :, k, :], x1[:])
 
             for i in range(PIECES):
-                piece = slice(i * W, (i + 1) * W)
+                piece = slice(CUTS[i], CUTS[i + 1])
                 for c in range(BLOCKS):
-                    sig1 = per_piece.tile([P, W], F32, name="sig1")
+                    sig1 = per_piece.tile([P, CUTS[i + 1] - CUTS[i]], F32, name="sig1")
                     nc.scalar.activation(sig1[:], sum1[c][i][:], SIGMOID, bias=b1_sb[:, c : c + 1])
-                    h1 = per_piece.tile([P, W], F32, name="h1")
+                    h1 = per_piece.tile([P, CUTS[i + 1] - CUTS[i]], F32, name="h1")
                     nc.vector.scalar_tensor_tensor(h1[:], sig1[:], 2.0, h_sb[:, c, piece], MULT, MULT)
                     nc.sync.dma_start(out_blocks[1, :, c, piece], h1[:])

@@ -22,13 +22,12 @@ def tile_luongattndecodermoglstm_kernel(tc, emb, h, w0, b0, w1, b1, offs, out):
         tc.tile_pool(name="per_block", bufs=BLOCKS) as per_block,
         tc.tile_pool(name="per_piece", bufs=BLOCKS * PIECES) as per_piece,
     ):
-        offsets = held.tile([P, N // 16], U16, name="offsets")
-        nc.sync.dma_start(offsets[:], offs)
-
         h_sb = held.tile([P, BLOCKS, N], BF16, name="h_sb")
         nc.sync.dma_start(h_sb[:], h.rearrange("(p b) j -> p b j", b=BLOCKS))
         w0_sb = held.tile([P, BLOCKS, P, BLOCKS], BF16, name="w0_sb")
         nc.sync.dma_start(w0_sb[:], w0.rearrange("(p k) (m c) -> p k m c", k=BLOCKS, c=BLOCKS))
+        offsets = held.tile([P, N // 16], U16, name="offsets")
+        nc.sync.dma_start(offsets[:], offs)
 
         b0_sb = held.tile([P, BLOCKS], F32, name="b0_sb")
         b1_sb = held.tile([P, BLOCKS], F32, name="b1_sb")
@@ -78,7 +77,10 @@ def tile_luongattndecodermoglstm_kernel(tc, emb, h, w0, b0, w1, b1, offs, out):
                     piece = slice(CUTS[i], CUTS[i + 1])
                     looked_up = emb_sb[k][:].indirect(offsets[:, CUTS[i] // 16 : CUTS[i + 1] // 16])
                     nc.vector.tensor_tensor(x1[:, piece], looked_up, q0[k][:, piece], MULT)
-                    nc.vector.tensor_copy(x1_bf[:, piece], x1[:, piece])
+                    if i == 0:
+                        nc.scalar.copy(x1_bf[:, piece], x1[:, piece])
+                    else:
+                        nc.vector.tensor_copy(x1_bf[:, piece], x1[:, piece])
                     for c in range(BLOCKS):
                         nc.tensor.matmul(
                             sum1[c][i][:],

@@ -1,4 +1,5 @@
 import concourse.mybir as mybir
+from concourse.masks import make_identity
 
 F32, BF16, U16 = mybir.dt.float32, mybir.dt.bfloat16, mybir.dt.uint16
 MULT = mybir.AluOpType.mult
@@ -9,6 +10,7 @@ C = 512
 S = 2048
 N = 256
 BLOCKS = C // P
+ROUNDS = 2
 PIECES = 2
 CUTS = [0, N // 4, N]
 
@@ -29,10 +31,11 @@ def tile_luongattndecodermoglstm_kernel(tc, emb, h, w0, b0, w1, b1, offs, out):
         offsets = held.tile([P, N // 16], U16, name="offsets")
         nc.sync.dma_start(offsets[:], offs)
 
-        b0_sb = held.tile([P, BLOCKS], F32, name="b0_sb")
-        b1_sb = held.tile([P, BLOCKS], F32, name="b1_sb")
-        nc.scalar.dma_start(b0_sb[:], b0.rearrange("(p b) o -> p (b o)", b=BLOCKS))
-        nc.scalar.dma_start(b1_sb[:], b1.rearrange("(p b) o -> p (b o)", b=BLOCKS))
+        bias_rows = held.tile([ROUNDS, P, BLOCKS], F32, name="bias_rows")
+        nc.scalar.dma_start(bias_rows[0:1], b0.rearrange("(m c) o -> o m c", c=BLOCKS))
+        nc.scalar.dma_start(bias_rows[1:2], b1.rearrange("(m c) o -> o m c", c=BLOCKS))
+        identity = held.tile([ROUNDS, ROUNDS], F32, name="identity")
+        make_identity(nc, identity[:])
 
         emb_blocks = emb.rearrange("(p b) s -> p b s", b=BLOCKS)
         emb_sb = [held.tile([P, S], F32, name=f"emb{b}") for b in range(BLOCKS)]
@@ -45,7 +48,14 @@ def tile_luongattndecodermoglstm_kernel(tc, emb, h, w0, b0, w1, b1, offs, out):
             nc.sync.dma_start(emb_sb[b][:], emb_blocks[:, b, :])
         nc.sync.dma_start(w1_sb[:, LAST], w1_blocks[:, LAST])
 
-        out_blocks = out.rearrange("(r p b) j -> r p b j", r=2, b=BLOCKS)
+        out_blocks = out.rearrange("(r p b) j -> r p b j", r=ROUNDS, b=BLOCKS)
+
+        bias = held.tile([P, BLOCKS, ROUNDS], F32, name="bias")
+        with tc.psum_pool(name="columns", bufs=1) as columns:
+            bias_columns = columns.tile([P, BLOCKS, ROUNDS], F32, name="bias_columns")
+            for c in range(BLOCKS):
+                nc.tensor.matmul(bias_columns[:, c, :], bias_rows[:, :, c], identity[:])
+            nc.vector.tensor_copy(bias[:], bias_columns[:])
 
         q0 = []
         with tc.psum_pool(name="sums0", bufs=2) as sums0:
@@ -60,7 +70,7 @@ def tile_luongattndecodermoglstm_kernel(tc, emb, h, w0, b0, w1, b1, offs, out):
                         stop=(k == BLOCKS - 1),
                     )
                 sig0 = per_block.tile([P, N], F32, name="sig0")
-                nc.scalar.activation(sig0[:], sum0[:], SIGMOID, bias=b0_sb[:, c : c + 1])
+                nc.scalar.activation(sig0[:], sum0[:], SIGMOID, bias=bias[:, c, 0:1])
                 q0_c = per_block.tile([P, N], F32, name="q0_c")
                 nc.vector.tensor_scalar_mul(q0_c[:], sig0[:], 2.0)
                 q0.append(q0_c)
@@ -95,7 +105,7 @@ def tile_luongattndecodermoglstm_kernel(tc, emb, h, w0, b0, w1, b1, offs, out):
                 piece = slice(CUTS[i], CUTS[i + 1])
                 for c in range(BLOCKS):
                     sig1 = per_piece.tile([P, CUTS[i + 1] - CUTS[i]], F32, name="sig1")
-                    nc.scalar.activation(sig1[:], sum1[c][i][:], SIGMOID, bias=b1_sb[:, c : c + 1])
+                    nc.scalar.activation(sig1[:], sum1[c][i][:], SIGMOID, bias=bias[:, c, 1:2])
                     h1 = per_piece.tile([P, CUTS[i + 1] - CUTS[i]], F32, name="h1")
                     nc.vector.scalar_tensor_tensor(h1[:], sig1[:], 2.0, h_sb[:, c, piece], MULT, MULT)
                     nc.sync.dma_start(out_blocks[1, :, c, piece], h1[:])

@@ -11,8 +11,8 @@ S = 2048
 N = 256
 BLOCKS = C // P
 ROUNDS = 2
-PIECES = 2
-CUTS = [0, N // 4, N]
+CUTS = [0, N // 4, N // 2, N]
+PIECES = len(CUTS) - 1
 
 FLOPS = 2 * (2 * C * C * N)
 
@@ -22,7 +22,7 @@ def tile_luongattndecodermoglstm_kernel(tc, emb, h, w0, b0, w1, b1, offs, out):
     with (
         tc.tile_pool(name="held", bufs=1) as held,
         tc.tile_pool(name="per_block", bufs=BLOCKS) as per_block,
-        tc.tile_pool(name="per_piece", bufs=BLOCKS * PIECES) as per_piece,
+        tc.tile_pool(name="per_piece", bufs=2 * BLOCKS) as per_piece,
     ):
         h_sb = held.tile([P, BLOCKS, N], BF16, name="h_sb")
         nc.sync.dma_start(h_sb[:], h.rearrange("(p b) j -> p b j", b=BLOCKS))
@@ -41,12 +41,13 @@ def tile_luongattndecodermoglstm_kernel(tc, emb, h, w0, b0, w1, b1, offs, out):
         emb_sb = [held.tile([P, S], F32, name=f"emb{b}") for b in range(BLOCKS)]
         w1_sb = held.tile([P, BLOCKS, P, BLOCKS], BF16, name="w1_sb")
         w1_blocks = w1.rearrange("(p k) (m c) -> p k m c", k=BLOCKS, c=BLOCKS)
-        LAST = BLOCKS - 1
+        EARLY = BLOCKS // 2
         nc.sync.dma_start(emb_sb[0][:], emb_blocks[:, 0, :])
-        nc.sync.dma_start(w1_sb[:, 0:LAST], w1_blocks[:, 0:LAST])
+        nc.sync.dma_start(w1_sb[:, 0:EARLY], w1_blocks[:, 0:EARLY])
         for b in range(1, BLOCKS):
             nc.sync.dma_start(emb_sb[b][:], emb_blocks[:, b, :])
-        nc.sync.dma_start(w1_sb[:, LAST], w1_blocks[:, LAST])
+        for b in range(EARLY, BLOCKS):
+            nc.sync.dma_start(w1_sb[:, b], w1_blocks[:, b])
 
         out_blocks = out.rearrange("(r p b) j -> r p b j", r=ROUNDS, b=BLOCKS)
 
@@ -76,10 +77,8 @@ def tile_luongattndecodermoglstm_kernel(tc, emb, h, w0, b0, w1, b1, offs, out):
                 q0.append(q0_c)
 
         with tc.psum_pool(name="sums1", bufs=1) as sums1:
-            sum1 = [
-                [sums1.tile([P, CUTS[i + 1] - CUTS[i]], F32, name=f"sum1_{c}_{i}") for i in range(PIECES)]
-                for c in range(BLOCKS)
-            ]
+            sums = [(c, 0, CUTS[1 + c // 2]) for c in range(BLOCKS)] + [(c, CUTS[1 + c // 2], N) for c in range(BLOCKS)]
+            sum1 = {(c, lo): sums1.tile([P, hi - lo], F32, name=f"sum1_{c}_{lo}") for c, lo, hi in sums}
             for k in range(BLOCKS):
                 x1 = per_block.tile([P, N], F32, name="x1")
                 x1_bf = per_block.tile([P, N], BF16, name="x1_bf")
@@ -87,25 +86,24 @@ def tile_luongattndecodermoglstm_kernel(tc, emb, h, w0, b0, w1, b1, offs, out):
                     piece = slice(CUTS[i], CUTS[i + 1])
                     looked_up = emb_sb[k][:].indirect(offsets[:, CUTS[i] // 16 : CUTS[i + 1] // 16])
                     nc.vector.tensor_tensor(x1[:, piece], looked_up, q0[k][:, piece], MULT)
-                    if i == 0:
+                    if i < PIECES - 1:
                         nc.scalar.copy(x1_bf[:, piece], x1[:, piece])
                     else:
                         nc.vector.tensor_copy(x1_bf[:, piece], x1[:, piece])
-                    for c in range(BLOCKS):
-                        nc.tensor.matmul(
-                            sum1[c][i][:],
-                            w1_sb[:, k, :, c],
-                            x1_bf[:, piece],
-                            start=(k == 0),
-                            stop=(k == BLOCKS - 1),
-                        )
+                    for c, lo, hi in sums:
+                        if hi == CUTS[i + 1]:
+                            nc.tensor.matmul(
+                                sum1[c, lo][:],
+                                w1_sb[:, k, :, c],
+                                x1_bf[:, lo:hi],
+                                start=(k == 0),
+                                stop=(k == BLOCKS - 1),
+                            )
                 nc.sync.dma_start(out_blocks[0, :, k, :], x1[:])
 
-            for i in range(PIECES):
-                piece = slice(CUTS[i], CUTS[i + 1])
-                for c in range(BLOCKS):
-                    sig1 = per_piece.tile([P, CUTS[i + 1] - CUTS[i]], F32, name="sig1")
-                    nc.scalar.activation(sig1[:], sum1[c][i][:], SIGMOID, bias=bias[:, c, 1:2])
-                    h1 = per_piece.tile([P, CUTS[i + 1] - CUTS[i]], F32, name="h1")
-                    nc.vector.scalar_tensor_tensor(h1[:], sig1[:], 2.0, h_sb[:, c, piece], MULT, MULT)
-                    nc.sync.dma_start(out_blocks[1, :, c, piece], h1[:])
+            for c, lo, hi in sums:
+                sig1 = per_piece.tile([P, hi - lo], F32, name="sig1")
+                nc.scalar.activation(sig1[:], sum1[c, lo][:], SIGMOID, bias=bias[:, c, 1:2])
+                h1 = per_piece.tile([P, hi - lo], F32, name="h1")
+                nc.vector.scalar_tensor_tensor(h1[:], sig1[:], 2.0, h_sb[:, c, lo:hi], MULT, MULT)
+                nc.sync.dma_start(out_blocks[1, :, c, lo:hi], h1[:])

@@ -10,6 +10,7 @@ C = 512
 S = 2048
 N = 256
 BLOCKS = C // P
+HALF = BLOCKS // 2
 ROUNDS = 2
 CUTS = [0, N // 4, N // 2, N]
 PIECES = len(CUTS) - 1
@@ -41,13 +42,13 @@ def tile_luongattndecodermoglstm_kernel(tc, emb, h, w0, b0, w1, b1, offs, out):
         emb_sb = [held.tile([P, S], F32, name=f"emb{b}") for b in range(BLOCKS)]
         w1_sb = held.tile([P, BLOCKS, P, BLOCKS], BF16, name="w1_sb")
         w1_blocks = w1.rearrange("(p k) (m c) -> p k m c", k=BLOCKS, c=BLOCKS)
-        EARLY = BLOCKS // 2
+        EARLY = 1
         nc.sync.dma_start(emb_sb[0][:], emb_blocks[:, 0, :])
         nc.sync.dma_start(w1_sb[:, 0:EARLY], w1_blocks[:, 0:EARLY])
         for b in range(1, BLOCKS):
             nc.sync.dma_start(emb_sb[b][:], emb_blocks[:, b, :])
-        for b in range(EARLY, BLOCKS):
-            nc.sync.dma_start(w1_sb[:, b], w1_blocks[:, b])
+        nc.sync.dma_start(w1_sb[:, EARLY:HALF], w1_blocks[:, EARLY:HALF])
+        nc.sync.dma_start(w1_sb[:, HALF:BLOCKS], w1_blocks[:, HALF:BLOCKS])
 
         out_blocks = out.rearrange("(r p b) j -> r p b j", r=ROUNDS, b=BLOCKS)
 
@@ -79,6 +80,7 @@ def tile_luongattndecodermoglstm_kernel(tc, emb, h, w0, b0, w1, b1, offs, out):
         with tc.psum_pool(name="sums1", bufs=1) as sums1:
             sums = [(c, 0, CUTS[1 + c // 2]) for c in range(BLOCKS)] + [(c, CUTS[1 + c // 2], N) for c in range(BLOCKS)]
             sum1 = {(c, lo): sums1.tile([P, hi - lo], F32, name=f"sum1_{c}_{lo}") for c, lo, hi in sums}
+            x1_bfs = []
             for k in range(BLOCKS):
                 x1 = per_block.tile([P, N], F32, name="x1")
                 x1_bf = per_block.tile([P, N], BF16, name="x1_bf")
@@ -90,16 +92,16 @@ def tile_luongattndecodermoglstm_kernel(tc, emb, h, w0, b0, w1, b1, offs, out):
                         nc.scalar.copy(x1_bf[:, piece], x1[:, piece])
                     else:
                         nc.vector.tensor_copy(x1_bf[:, piece], x1[:, piece])
-                    for c, lo, hi in sums:
-                        if hi == CUTS[i + 1]:
-                            nc.tensor.matmul(
-                                sum1[c, lo][:],
-                                w1_sb[:, k, :, c],
-                                x1_bf[:, lo:hi],
-                                start=(k == 0),
-                                stop=(k == BLOCKS - 1),
-                            )
                 nc.sync.dma_start(out_blocks[0, :, k, :], x1[:])
+                x1_bfs.append(x1_bf)
+                if k < HALF:
+                    for c, lo, hi in sums:
+                        nc.tensor.matmul(sum1[c, lo][:], w1_sb[:, k, :, c], x1_bf[:, lo:hi], start=(k == 0), stop=False)
+            for c, lo, hi in sums:
+                for k in range(HALF, BLOCKS):
+                    nc.tensor.matmul(
+                        sum1[c, lo][:], w1_sb[:, k, :, c], x1_bfs[k][:, lo:hi], start=False, stop=(k == BLOCKS - 1)
+                    )
 
             for c, lo, hi in sums:
                 sig1 = per_piece.tile([P, hi - lo], F32, name="sig1")

@@ -42,11 +42,13 @@ def tile_luongattndecodermoglstm_kernel(tc, emb, h, w0, b0, w1, b1, offs, out):
         emb_sb = [held.tile([P, S], F32, name=f"emb{b}") for b in range(BLOCKS)]
         w1_sb = held.tile([P, BLOCKS, P, BLOCKS], BF16, name="w1_sb")
         w1_blocks = w1.rearrange("(p k) (m c) -> p k m c", k=BLOCKS, c=BLOCKS)
+        LAST = BLOCKS - 1
         EARLY = 1
         nc.sync.dma_start(emb_sb[0][:], emb_blocks[:, 0, :])
-        nc.sync.dma_start(w1_sb[:, 0:EARLY], w1_blocks[:, 0:EARLY])
-        for b in range(1, BLOCKS):
+        for b in range(1, LAST):
             nc.sync.dma_start(emb_sb[b][:], emb_blocks[:, b, :])
+        nc.sync.dma_start(w1_sb[:, 0:EARLY], w1_blocks[:, 0:EARLY])
+        nc.sync.dma_start(emb_sb[LAST][:], emb_blocks[:, LAST, :])
         nc.sync.dma_start(w1_sb[:, EARLY:HALF], w1_blocks[:, EARLY:HALF])
         nc.sync.dma_start(w1_sb[:, HALF:BLOCKS], w1_blocks[:, HALF:BLOCKS])
 

import concourse.mybir as mybir
from concourse.masks import make_identity

F32, BF16, U16 = mybir.dt.float32, mybir.dt.bfloat16, mybir.dt.uint16
MULT = mybir.AluOpType.mult
SIGMOID = mybir.ActivationFunctionType.Sigmoid

P = 128
C = 512
S = 2048
N = 256
BLOCKS = C // P
HALF = BLOCKS // 2
ROUNDS = 2
CUTS = [0, N // 4, N // 2, N]
PIECES = len(CUTS) - 1

FLOPS = 2 * (2 * C * C * N)


def tile_luongattndecodermoglstm_kernel(tc, emb, h, w0, b0, w1, b1, offs, out):
    nc = tc.nc
    with (
        tc.tile_pool(name="held", bufs=1) as held,
        tc.tile_pool(name="per_block", bufs=BLOCKS) as per_block,
        tc.tile_pool(name="per_piece", bufs=2 * BLOCKS) as per_piece,
    ):
        h_sb = held.tile([P, BLOCKS, N], BF16, name="h_sb")
        nc.sync.dma_start(h_sb[:], h.rearrange("(p b) j -> p b j", b=BLOCKS))
        w0_sb = held.tile([P, BLOCKS, P, BLOCKS], BF16, name="w0_sb")
        nc.sync.dma_start(w0_sb[:], w0.rearrange("(p k) (m c) -> p k m c", k=BLOCKS, c=BLOCKS))
        offsets = held.tile([P, N // 16], U16, name="offsets")
        nc.sync.dma_start(offsets[:], offs)

        bias_rows = held.tile([ROUNDS, P, BLOCKS], F32, name="bias_rows")
        nc.scalar.dma_start(bias_rows[0:1], b0.rearrange("(m c) o -> o m c", c=BLOCKS))
        nc.scalar.dma_start(bias_rows[1:2], b1.rearrange("(m c) o -> o m c", c=BLOCKS))
        identity = held.tile([ROUNDS, ROUNDS], F32, name="identity")
        make_identity(nc, identity[:])

        emb_blocks = emb.rearrange("(p b) s -> p b s", b=BLOCKS)
        emb_sb = [held.tile([P, S], F32, name=f"emb{b}") for b in range(BLOCKS)]
        w1_sb = held.tile([P, BLOCKS, P, BLOCKS], BF16, name="w1_sb")
        w1_blocks = w1.rearrange("(p k) (m c) -> p k m c", k=BLOCKS, c=BLOCKS)
        LAST = BLOCKS - 1
        EARLY = 1
        nc.sync.dma_start(emb_sb[0][:], emb_blocks[:, 0, :])
        for b in range(1, LAST):
            nc.sync.dma_start(emb_sb[b][:], emb_blocks[:, b, :])
        nc.sync.dma_start(w1_sb[:, 0:EARLY], w1_blocks[:, 0:EARLY])
        nc.sync.dma_start(emb_sb[LAST][:], emb_blocks[:, LAST, :])
        nc.sync.dma_start(w1_sb[:, EARLY:HALF], w1_blocks[:, EARLY:HALF])
        nc.sync.dma_start(w1_sb[:, HALF:BLOCKS], w1_blocks[:, HALF:BLOCKS])

        out_blocks = out.rearrange("(r p b) j -> r p b j", r=ROUNDS, b=BLOCKS)

        bias = held.tile([P, BLOCKS, ROUNDS], F32, name="bias")
        with tc.psum_pool(name="columns", bufs=1) as columns:
            bias_columns = columns.tile([P, BLOCKS, ROUNDS], F32, name="bias_columns")
            for c in range(BLOCKS):
                nc.tensor.matmul(bias_columns[:, c, :], bias_rows[:, :, c], identity[:])
            nc.vector.tensor_copy(bias[:], bias_columns[:])

        q0 = []
        with tc.psum_pool(name="sums0", bufs=2) as sums0:
            for c in range(BLOCKS):
                sum0 = sums0.tile([P, N], F32, name="sum0")
                for k in range(BLOCKS):
                    nc.tensor.matmul(
                        sum0[:],
                        w0_sb[:, k, :, c],
                        h_sb[:, k, :],
                        start=(k == 0),
                        stop=(k == BLOCKS - 1),
                    )
                sig0 = per_block.tile([P, N], F32, name="sig0")
                nc.scalar.activation(sig0[:], sum0[:], SIGMOID, bias=bias[:, c, 0:1])
                q0_c = per_block.tile([P, N], F32, name="q0_c")
                nc.vector.tensor_scalar_mul(q0_c[:], sig0[:], 2.0)
                q0.append(q0_c)

        with tc.psum_pool(name="sums1", bufs=1) as sums1:
            sums = [(c, 0, CUTS[1 + c // 2]) for c in range(BLOCKS)] + [(c, CUTS[1 + c // 2], N) for c in range(BLOCKS)]
            sum1 = {(c, lo): sums1.tile([P, hi - lo], F32, name=f"sum1_{c}_{lo}") for c, lo, hi in sums}
            x1_bfs = []
            for k in range(BLOCKS):
                x1 = per_block.tile([P, N], F32, name="x1")
                x1_bf = per_block.tile([P, N], BF16, name="x1_bf")
                for i in range(PIECES):
                    piece = slice(CUTS[i], CUTS[i + 1])
                    looked_up = emb_sb[k][:].indirect(offsets[:, CUTS[i] // 16 : CUTS[i + 1] // 16])
                    nc.vector.tensor_tensor(x1[:, piece], looked_up, q0[k][:, piece], MULT)
                    if i < PIECES - 1:
                        nc.scalar.copy(x1_bf[:, piece], x1[:, piece])
                    else:
                        nc.vector.tensor_copy(x1_bf[:, piece], x1[:, piece])
                nc.sync.dma_start(out_blocks[0, :, k, :], x1[:])
                x1_bfs.append(x1_bf)
                if k < HALF:
                    for c, lo, hi in sums:
                        nc.tensor.matmul(sum1[c, lo][:], w1_sb[:, k, :, c], x1_bf[:, lo:hi], start=(k == 0), stop=False)
            for c, lo, hi in sums:
                for k in range(HALF, BLOCKS):
                    nc.tensor.matmul(
                        sum1[c, lo][:], w1_sb[:, k, :, c], x1_bfs[k][:, lo:hi], start=False, stop=(k == BLOCKS - 1)
                    )

            for c, lo, hi in sums:
                sig1 = per_piece.tile([P, hi - lo], F32, name="sig1")
                nc.scalar.activation(sig1[:], sum1[c, lo][:], SIGMOID, bias=bias[:, c, 1:2])
                h1 = per_piece.tile([P, hi - lo], F32, name="h1")
                nc.vector.scalar_tensor_tensor(h1[:], sig1[:], 2.0, h_sb[:, c, lo:hi], MULT, MULT)
                nc.sync.dma_start(out_blocks[1, :, c, lo:hi], h1[:])
